import numpy as np
import ml_dtypes


def mxq(x, axis, fmt="e4m3"):
    dtype, down = {"e4m3": (ml_dtypes.float8_e4m3fn, 7), "e5m2": (ml_dtypes.float8_e5m2, 14)}[fmt]
    v = np.moveaxis(np.asarray(x, np.float32).astype(ml_dtypes.bfloat16).astype(np.float64), axis, -1)
    blocks = v.reshape(v.shape[:-1] + (-1, 32))
    amax = np.abs(blocks).max(-1, keepdims=True)
    byte = np.maximum(np.where(amax > 0, np.frexp(amax)[1] - 1 + 127, 0) - down, 1)
    scale = np.exp2(byte - 127.0)
    codes = (blocks / scale).astype(np.float32).astype(dtype).astype(np.float64)
    return np.moveaxis((codes * scale).reshape(v.shape), -1, axis)


WIDE = False


def mx_kscale(k):
    if not WIDE:
        return np.ones(k)
    levels = np.array([20, -20, 10, -10, 0])
    a = np.random.permutation(np.resize(levels, k // 512 * 4)).reshape(k // 512, 4)
    idx = np.arange(k)
    return np.exp2(a[idx // 512, idx % 128 // 32])


BF16 = ml_dtypes.bfloat16


def bf(x):
    return np.asarray(x, np.float32).astype(BF16)


def f64(x):
    return np.asarray(x).astype(np.float64)


B, IMG, P0, P1, C, F = 2, 512, 8, 16, 2, 512
E0, E1 = IMG // P0, IMG // P1
N0, N1 = E0 * E0, E1 * E1
D0, D1 = P0 * P0 * C, P1 * P1 * C
T = B * N1


def repatch(encoded):
    x = encoded.reshape(-1, E0, E0, P0, P0, C)
    img = x.transpose(0, 1, 3, 2, 4, 5).reshape(-1, IMG, IMG, C)
    new_patches = img.reshape(-1, E1, P1, E1, P1, C).transpose(0, 1, 3, 2, 4, 5)
    return new_patches.reshape(-1, N1, D1)


def setup_inputs():
    s = mx_kscale(T).reshape(B, N1, 1)
    flat = np.random.standard_normal((B, N1, D1)) * s
    img = flat.reshape(B, E1, E1, P1, P1, C).transpose(0, 1, 3, 2, 4, 5).reshape(B, IMG, IMG, C)
    encoded = img.reshape(B, E0, P0, E0, P0, C).transpose(0, 1, 3, 2, 4, 5).reshape(B, N0, D0)
    W = np.random.standard_normal((D1, F)) / np.sqrt(D1)
    b = np.random.standard_normal(F) * 0.3
    pos_emb = np.random.standard_normal((N1, F)) * 0.5
    g = np.random.standard_normal((B, N1, F)) * np.exp2(np.random.randint(-12, 1, (B, N1, 1))) / s
    return {"encoded": bf(encoded), "W": bf(W), "b": bf(b), "pos_emb": bf(pos_emb), "grad_out": bf(g)}


def reference(encoded, W, b, pos_emb, grad_out):
    flat = repatch(f64(encoded)).reshape(T, D1)
    g = f64(grad_out).reshape(T, F)
    return mxq(flat, 0, "e4m3").T @ mxq(g, 0, "e5m2")

@@ -1,0 +1,86 @@
+from contextlib import ExitStack
+
+import concourse.mybir as mybir
+
+BF16 = mybir.dt.bfloat16
+F32 = mybir.dt.float32
+U32 = mybir.dt.uint32
+U8 = mybir.dt.uint8
+E4M3X4 = mybir.dt.float8_e4m3fn_x4
+E5M2X4 = mybir.dt.float8_e5m2_x4
+
+P = 128
+PACK = 4
+PASSES = 4
+D1 = 512
+F = 512
+
+FLOPS = 2 * 2048 * 512 * 512
+BYTES = 2 * 2048 * 512 * 2 + 512 * 512 * 4
+
+
+def tile_resampling_kernel(tc, encoded, W, b, pos_emb, grad_out, out):
+    nc = tc.nc
+    with ExitStack() as ctx:
+        keep = ctx.enter_context(tc.tile_pool(name="keep", bufs=1))
+        psum = ctx.enter_context(tc.psum_pool(name="acc", bufs=1))
+
+        enc_v = encoded.rearrange(
+            "i (h y a x r) c -> i h a y x (r c)", h=2, y=16, a=2, x=8, r=8
+        )
+        g_v = grad_out.flatten_outer_dims().rearrange("(c p j) e -> c p (j e)", p=P, j=PACK)
+
+        f_raw = [keep.tile([P, 2, 1024], BF16, name="f_raw%d" % c) for c in range(PASSES)]
+        g_raw = [keep.tile([P, 2048], BF16, name="g_raw%d" % c) for c in range(PASSES)]
+        f_grp = [keep.tile([P, 2048], BF16, name="f_grp%d" % c, align_bytes=64) for c in range(PASSES)]
+        g_grp = [keep.tile([P, 2048], BF16, name="g_grp%d" % c, align_bytes=64) for c in range(PASSES)]
+        f_cod = [keep.tile([P, D1], U32, name="f_cod%d" % c, align_bytes=64) for c in range(PASSES)]
+        g_cod = [keep.tile([P, F], U32, name="g_cod%d" % c, align_bytes=64) for c in range(PASSES)]
+        f_scl = [keep.tile([P, D1], U8, name="f_scl%d" % c, align_bytes=64) for c in range(PASSES)]
+        g_scl = [keep.tile([P, F], U8, name="g_scl%d" % c, align_bytes=64) for c in range(PASSES)]
+        acc = [psum.tile([P, F], F32, name="acc%d" % m) for m in range(4)]
+        res = [keep.tile([P, F], F32, name="res%d" % m) for m in range(4)]
+
+        for c in range(PASSES):
+            nc.sync.dma_start(out=g_raw[c][:], in_=g_v[c])
+            for a in range(2):
+                nc.sync.dma_start(out=f_raw[c][:, a, :], in_=enc_v[c // 2, c % 2, a])
+
+        for c in range(PASSES):
+            nc.scalar.copy(
+                out=g_grp[c][:].rearrange("p (q i j) -> p q j i", i=4, j=PACK),
+                in_=g_raw[c][:].rearrange("p (j q i) -> p q j i", i=4, j=PACK),
+            )
+            for a in range(2):
+                dst = f_grp[c][:, a * 1024 : (a + 1) * 1024].rearrange(
+                    "p (r b q i j) -> p b r q j i", r=8, b=2, q=4, i=4, j=PACK
+                )
+                src = f_raw[c][:, a, :].rearrange(
+                    "p (j b r q i) -> p b r q j i", r=8, b=2, q=4, i=4, j=PACK
+                )
+                for bb in range(2):
+                    nc.vector.tensor_copy(out=dst[:, bb], in_=src[:, bb])
+            nc.vector.quantize_mx(
+                out=g_cod[c][:].bitcast(E5M2X4), scales=g_scl[c][:], in_=g_grp[c][:]
+            )
+            nc.vector.quantize_mx(
+                out=f_cod[c][:].bitcast(E4M3X4), scales=f_scl[c][:], in_=f_grp[c][:]
+            )
+            for m in range(4):
+                cols = slice(m * P, (m + 1) * P)
+                nc.tensor.matmul_mx(
+                    out=acc[m][:],
+                    lhsT=f_cod[c][:, cols].bitcast(E4M3X4),
+                    lhsT_scale=f_scl[c][:, cols],
+                    rhs=g_cod[c][:].bitcast(E5M2X4),
+                    rhs_scale=g_scl[c][:],
+                    start=(c == 0),
+                    stop=(c == PASSES - 1),
+                )
+
+        for m in range(4):
+            if m % 2 == 0:
+                nc.scalar.copy(out=res[m][:], in_=acc[m][:])
+            else:
+                nc.vector.tensor_copy(out=res[m][:], in_=acc[m][:])
+            nc.sync.dma_start(out=out[m * P : (m + 1) * P, :], in_=res[m][:])

@@ -18,12 +18,20 @@ F = 512
 FLOPS = 2 * 2048 * 512 * 512
 BYTES = 2 * 2048 * 512 * 2 + 512 * 512 * 4
 
+PINNED = True
+LOADS = (
+    ("f", 0, 0), ("g", 0, 0), ("f", 1, 0), ("g", 1, 0), ("f", 2, 0), ("g", 2, 0), ("f", 3, 0), ("g", 3, 0),
+    ("f", 0, 1), ("f", 1, 1), ("f", 2, 1), ("f", 3, 1),
+)
+
 
 def tile_resampling_kernel(tc, encoded, W, b, pos_emb, grad_out, out):
     nc = tc.nc
     with ExitStack() as ctx:
         keep = ctx.enter_context(tc.tile_pool(name="keep", bufs=1))
         psum = ctx.enter_context(tc.psum_pool(name="acc", bufs=1))
+        if PINNED:
+            ctx.enter_context(tc.manual_schedule())
 
         enc_v = encoded.rearrange(
             "i (h y a x r) c -> i h a y x (r c)", h=2, y=16, a=2, x=8, r=8
@@ -41,32 +49,50 @@ def tile_resampling_kernel(tc, encoded, W, b, pos_emb, grad_out, out):
         acc = [psum.tile([P, F], F32, name="acc%d" % m) for m in range(4)]
         res = [keep.tile([P, F], F32, name="res%d" % m) for m in range(4)]
 
-        for c in range(PASSES):
-            nc.sync.dma_start(out=g_raw[c][:], in_=g_v[c])
-            for a in range(2):
+        for kind, c, a in LOADS:
+            if kind == "g":
+                nc.sync.dma_start(out=g_raw[c][:], in_=g_v[c])
+            else:
                 nc.sync.dma_start(out=f_raw[c][:, a, :], in_=enc_v[c // 2, c % 2, a])
 
-        for c in range(PASSES):
-            nc.scalar.copy(
-                out=g_grp[c][:].rearrange("p (q i j) -> p q j i", i=4, j=PACK),
-                in_=g_raw[c][:].rearrange("p (j q i) -> p q j i", i=4, j=PACK),
-            )
-            for a in range(2):
+        def regroup(kind, c, a):
+            if kind == "g":
+                src = g_raw[c][:].rearrange("p (j e) -> p j e", j=PACK)
+                for half, copy in ((0, nc.vector.tensor_copy), (1, nc.scalar.copy)):
+                    copy(
+                        out=g_grp[c][:, half * 1024 : (half + 1) * 1024].rearrange(
+                            "p (q i j) -> p q j i", i=4, j=PACK
+                        ),
+                        in_=src[:, :, half * 256 : (half + 1) * 256].rearrange(
+                            "p j (q i) -> p q j i", i=4
+                        ),
+                    )
+            else:
                 dst = f_grp[c][:, a * 1024 : (a + 1) * 1024].rearrange(
                     "p (r b q i j) -> p b r q j i", r=8, b=2, q=4, i=4, j=PACK
                 )
                 src = f_raw[c][:, a, :].rearrange(
                     "p (j b r q i) -> p b r q j i", r=8, b=2, q=4, i=4, j=PACK
                 )
-                for bb in range(2):
-                    nc.vector.tensor_copy(out=dst[:, bb], in_=src[:, bb])
-            nc.vector.quantize_mx(
-                out=g_cod[c][:].bitcast(E5M2X4), scales=g_scl[c][:], in_=g_grp[c][:]
-            )
-            nc.vector.quantize_mx(
-                out=f_cod[c][:].bitcast(E4M3X4), scales=f_scl[c][:], in_=f_grp[c][:]
-            )
-            for m in range(4):
+                nc.vector.tensor_copy(out=dst[:, 0], in_=src[:, 0])
+                nc.scalar.copy(out=dst[:, 1], in_=src[:, 1])
+
+        def quantise(kind, c, a):
+            if kind == "g":
+                nc.vector.quantize_mx(
+                    out=g_cod[c][:].bitcast(E5M2X4), scales=g_scl[c][:], in_=g_grp[c][:]
+                )
+            else:
+                nc.vector.quantize_mx(
+                    out=f_cod[c][:, a * 256 : (a + 1) * 256].bitcast(E4M3X4),
+                    scales=f_scl[c][:, a * 256 : (a + 1) * 256],
+                    in_=f_grp[c][:, a * 1024 : (a + 1) * 1024],
+                )
+
+        count = [0, 0, 0, 0]
+
+        def multiply(c, a):
+            for m in (2 * a, 2 * a + 1):
                 cols = slice(m * P, (m + 1) * P)
                 nc.tensor.matmul_mx(
                     out=acc[m][:],
@@ -74,12 +100,33 @@ def tile_resampling_kernel(tc, encoded, W, b, pos_emb, grad_out, out):
                     lhsT_scale=f_scl[c][:, cols],
                     rhs=g_cod[c][:].bitcast(E5M2X4),
                     rhs_scale=g_scl[c][:],
-                    start=(c == 0),
-                    stop=(c == PASSES - 1),
+                    start=(count[m] == 0),
+                    stop=(count[m] == PASSES - 1),
                 )
+                count[m] += 1
+
+        ready = set()
+        multiplied = set()
+
+        def finish(item):
+            quantise(item[0], item[1], item[2])
+            ready.add(item)
+            for c in range(PASSES):
+                for a in range(2):
+                    if ("g", c, 0) in ready and ("f", c, a) in ready and (c, a) not in multiplied:
+                        multiplied.add((c, a))
+                        multiply(c, a)
+
+        previous = None
+        for item in LOADS:
+            regroup(item[0], item[1], item[2])
+            if previous is not None:
+                finish(previous)
+            previous = item
+        finish(previous)
 
         for m in range(4):
-            if m % 2 == 0:
+            if m < 3:
                 nc.scalar.copy(out=res[m][:], in_=acc[m][:])
             else:
                 nc.vector.tensor_copy(out=res[m][:], in_=acc[m][:])

@@ -18,10 +18,19 @@ F = 512
 FLOPS = 2 * 2048 * 512 * 512
 BYTES = 2 * 2048 * 512 * 2 + 512 * 512 * 4
 
-PINNED = True
 LOADS = (
-    ("f", 0, 0), ("g", 0, 0), ("f", 1, 0), ("g", 1, 0), ("f", 2, 0), ("g", 2, 0), ("f", 3, 0), ("g", 3, 0),
-    ("f", 0, 1), ("f", 1, 1), ("f", 2, 1), ("f", 3, 1),
+    ("f", 0, 0),
+    ("g", 0, 0),
+    ("f", 0, 1),
+    ("f", 1, 0),
+    ("g", 1, 0),
+    ("f", 1, 1),
+    ("f", 2, 0),
+    ("g", 2, 0),
+    ("f", 3, 0),
+    ("g", 3, 0),
+    ("f", 2, 1),
+    ("f", 3, 1),
 )
 
 
@@ -30,8 +39,7 @@ def tile_resampling_kernel(tc, encoded, W, b, pos_emb, grad_out, out):
     with ExitStack() as ctx:
         keep = ctx.enter_context(tc.tile_pool(name="keep", bufs=1))
         psum = ctx.enter_context(tc.psum_pool(name="acc", bufs=1))
-        if PINNED:
-            ctx.enter_context(tc.manual_schedule())
+        ctx.enter_context(tc.manual_schedule())
 
         enc_v = encoded.rearrange(
             "i (h y a x r) c -> i h a y x (r c)", h=2, y=16, a=2, x=8, r=8
@@ -55,75 +63,92 @@ def tile_resampling_kernel(tc, encoded, W, b, pos_emb, grad_out, out):
             else:
                 nc.sync.dma_start(out=f_raw[c][:, a, :], in_=enc_v[c // 2, c % 2, a])
 
-        def regroup(kind, c, a):
-            if kind == "g":
-                src = g_raw[c][:].rearrange("p (j e) -> p j e", j=PACK)
-                for half, copy in ((0, nc.vector.tensor_copy), (1, nc.scalar.copy)):
-                    copy(
-                        out=g_grp[c][:, half * 1024 : (half + 1) * 1024].rearrange(
-                            "p (q i j) -> p q j i", i=4, j=PACK
-                        ),
-                        in_=src[:, :, half * 256 : (half + 1) * 256].rearrange(
-                            "p j (q i) -> p q j i", i=4
-                        ),
-                    )
-            else:
-                dst = f_grp[c][:, a * 1024 : (a + 1) * 1024].rearrange(
-                    "p (r b q i j) -> p b r q j i", r=8, b=2, q=4, i=4, j=PACK
-                )
-                src = f_raw[c][:, a, :].rearrange(
-                    "p (j b r q i) -> p b r q j i", r=8, b=2, q=4, i=4, j=PACK
-                )
-                nc.vector.tensor_copy(out=dst[:, 0], in_=src[:, 0])
-                nc.scalar.copy(out=dst[:, 1], in_=src[:, 1])
+        def regroup_g(copy, c, lo, hi):
+            copy(
+                out=g_grp[c][:, lo * PACK : hi * PACK].rearrange("p (q i j) -> p q j i", i=4, j=PACK),
+                in_=g_raw[c][:].rearrange("p (j e) -> p j e", j=PACK)[:, :, lo:hi].rearrange(
+                    "p j (q i) -> p q j i", i=4
+                ),
+            )
 
-        def quantise(kind, c, a):
-            if kind == "g":
-                nc.vector.quantize_mx(
-                    out=g_cod[c][:].bitcast(E5M2X4), scales=g_scl[c][:], in_=g_grp[c][:]
-                )
-            else:
-                nc.vector.quantize_mx(
-                    out=f_cod[c][:, a * 256 : (a + 1) * 256].bitcast(E4M3X4),
-                    scales=f_scl[c][:, a * 256 : (a + 1) * 256],
-                    in_=f_grp[c][:, a * 1024 : (a + 1) * 1024],
-                )
+        def regroup_f(copy, c, a, bb, r_lo, r_hi):
+            dst = f_grp[c][:, a * 1024 : (a + 1) * 1024].rearrange(
+                "p (r b q i j) -> p b r q j i", r=8, b=2, q=4, i=4, j=PACK
+            )
+            src = f_raw[c][:, a, :].rearrange(
+                "p (j b r q i) -> p b r q j i", r=8, b=2, q=4, i=4, j=PACK
+            )
+            copy(out=dst[:, bb, r_lo:r_hi], in_=src[:, bb, r_lo:r_hi])
+
+        def quantise_g(c):
+            nc.vector.quantize_mx(
+                out=g_cod[c][:].bitcast(E5M2X4), scales=g_scl[c][:], in_=g_grp[c][:]
+            )
+
+        def quantise_f(c, lo, hi):
+            nc.vector.quantize_mx(
+                out=f_cod[c][:, lo:hi].bitcast(E4M3X4),
+                scales=f_scl[c][:, lo:hi],
+                in_=f_grp[c][:, lo * PACK : hi * PACK],
+            )
 
         count = [0, 0, 0, 0]
 
-        def multiply(c, a):
-            for m in (2 * a, 2 * a + 1):
-                cols = slice(m * P, (m + 1) * P)
-                nc.tensor.matmul_mx(
-                    out=acc[m][:],
-                    lhsT=f_cod[c][:, cols].bitcast(E4M3X4),
-                    lhsT_scale=f_scl[c][:, cols],
-                    rhs=g_cod[c][:].bitcast(E5M2X4),
-                    rhs_scale=g_scl[c][:],
-                    start=(count[m] == 0),
-                    stop=(count[m] == PASSES - 1),
-                )
-                count[m] += 1
+        def multiply(c, m):
+            cols = slice(m * P, (m + 1) * P)
+            nc.tensor.matmul_mx(
+                out=acc[m][:],
+                lhsT=f_cod[c][:, cols].bitcast(E4M3X4),
+                lhsT_scale=f_scl[c][:, cols],
+                rhs=g_cod[c][:].bitcast(E5M2X4),
+                rhs_scale=g_scl[c][:],
+                start=(count[m] == 0),
+                stop=(count[m] == PASSES - 1),
+            )
+            count[m] += 1
 
         ready = set()
         multiplied = set()
 
         def finish(item):
-            quantise(item[0], item[1], item[2])
+            if item[0] == "g":
+                quantise_g(item[1])
+            else:
+                quantise_f(item[1], item[2] * 256, item[2] * 256 + 256)
             ready.add(item)
             for c in range(PASSES):
                 for a in range(2):
                     if ("g", c, 0) in ready and ("f", c, a) in ready and (c, a) not in multiplied:
                         multiplied.add((c, a))
-                        multiply(c, a)
+                        multiply(c, 2 * a)
+                        multiply(c, 2 * a + 1)
 
         previous = None
-        for item in LOADS:
-            regroup(item[0], item[1], item[2])
-            if previous is not None:
-                finish(previous)
-            previous = item
+        for n, item in enumerate(LOADS[:-1]):
+            kind, c, a = item
+            if kind == "g":
+                regroup_g(nc.vector.tensor_copy, c, 0, 256)
+                regroup_g(nc.scalar.copy, c, 256, 512)
+            else:
+                regroup_f(nc.vector.tensor_copy, c, a, 0, 0, 8)
+                regroup_f(nc.scalar.copy, c, a, 1, 0, 8)
+            if n == 0:
+                finish(item)
+            else:
+                if previous is not None:
+                    finish(previous)
+                previous = item
+
+        kind, c, a = LOADS[-1]
+        regroup_f(nc.vector.tensor_copy, c, a, 0, 0, 4)
+        regroup_f(nc.vector.tensor_copy, c, a, 1, 0, 4)
+        regroup_f(nc.scalar.copy, c, a, 1, 4, 8)
         finish(previous)
+        quantise_f(c, a * 256, a * 256 + 128)
+        multiply(c, 2 * a)
+        regroup_f(nc.vector.tensor_copy, c, a, 0, 4, 8)
+        quantise_f(c, a * 256 + 128, a * 256 + 256)
+        multiply(c, 2 * a + 1)
 
         for m in range(4):
             if m < 3:

@@ -18,19 +18,10 @@ F = 512
 FLOPS = 2 * 2048 * 512 * 512
 BYTES = 2 * 2048 * 512 * 2 + 512 * 512 * 4
 
+PINNED = True
 LOADS = (
-    ("f", 0, 0),
-    ("g", 0, 0),
-    ("f", 0, 1),
-    ("f", 1, 0),
-    ("g", 1, 0),
-    ("f", 1, 1),
-    ("f", 2, 0),
-    ("g", 2, 0),
-    ("f", 3, 0),
-    ("g", 3, 0),
-    ("f", 2, 1),
-    ("f", 3, 1),
+    ("f", 0, 0), ("g", 0, 0), ("f", 1, 0), ("g", 1, 0), ("f", 2, 0), ("g", 2, 0), ("f", 3, 0), ("g", 3, 0),
+    ("f", 0, 1), ("f", 1, 1), ("f", 2, 1), ("f", 3, 1),
 )
 
 
@@ -39,7 +30,8 @@ def tile_resampling_kernel(tc, encoded, W, b, pos_emb, grad_out, out):
     with ExitStack() as ctx:
         keep = ctx.enter_context(tc.tile_pool(name="keep", bufs=1))
         psum = ctx.enter_context(tc.psum_pool(name="acc", bufs=1))
-        ctx.enter_context(tc.manual_schedule())
+        if PINNED:
+            ctx.enter_context(tc.manual_schedule())
 
         enc_v = encoded.rearrange(
             "i (h y a x r) c -> i h a y x (r c)", h=2, y=16, a=2, x=8, r=8
@@ -63,96 +55,84 @@ def tile_resampling_kernel(tc, encoded, W, b, pos_emb, grad_out, out):
             else:
                 nc.sync.dma_start(out=f_raw[c][:, a, :], in_=enc_v[c // 2, c % 2, a])
 
-        def regroup_g(copy, c, lo, hi):
-            copy(
-                out=g_grp[c][:, lo * PACK : hi * PACK].rearrange("p (q i j) -> p q j i", i=4, j=PACK),
-                in_=g_raw[c][:].rearrange("p (j e) -> p j e", j=PACK)[:, :, lo:hi].rearrange(
-                    "p j (q i) -> p q j i", i=4
-                ),
-            )
+        def regroup(kind, c, a):
+            if kind == "g":
+                src = g_raw[c][:].rearrange("p (j e) -> p j e", j=PACK)
+                for half, copy in ((0, nc.vector.tensor_copy), (1, nc.scalar.copy)):
+                    copy(
+                        out=g_grp[c][:, half * 1024 : (half + 1) * 1024].rearrange(
+                            "p (q i j) -> p q j i", i=4, j=PACK
+                        ),
+                        in_=src[:, :, half * 256 : (half + 1) * 256].rearrange(
+                            "p j (q i) -> p q j i", i=4
+                        ),
+                    )
+            else:
+                dst = f_grp[c][:, a * 1024 : (a + 1) * 1024].rearrange(
+                    "p (r b q i j) -> p b r q j i", r=8, b=2, q=4, i=4, j=PACK
+                )
+                src = f_raw[c][:, a, :].rearrange(
+                    "p (j b r q i) -> p b r q j i", r=8, b=2, q=4, i=4, j=PACK
+                )
+                nc.vector.tensor_copy(out=dst[:, 0], in_=src[:, 0])
+                nc.scalar.copy(out=dst[:, 1], in_=src[:, 1])
 
-        def regroup_f(copy, c, a, bb, r_lo, r_hi):
-            dst = f_grp[c][:, a * 1024 : (a + 1) * 1024].rearrange(
-                "p (r b q i j) -> p b r q j i", r=8, b=2, q=4, i=4, j=PACK
-            )
-            src = f_raw[c][:, a, :].rearrange(
-                "p (j b r q i) -> p b r q j i", r=8, b=2, q=4, i=4, j=PACK
-            )
-            copy(out=dst[:, bb, r_lo:r_hi], in_=src[:, bb, r_lo:r_hi])
-
-        def quantise_g(c):
-            nc.vector.quantize_mx(
-                out=g_cod[c][:].bitcast(E5M2X4), scales=g_scl[c][:], in_=g_grp[c][:]
-            )
-
-        def quantise_f(c, lo, hi):
-            nc.vector.quantize_mx(
-                out=f_cod[c][:, lo:hi].bitcast(E4M3X4),
-                scales=f_scl[c][:, lo:hi],
-                in_=f_grp[c][:, lo * PACK : hi * PACK],
-            )
+        def quantise(kind, c, a):
+            if kind == "g":
+                nc.vector.quantize_mx(
+                    out=g_cod[c][:].bitcast(E5M2X4), scales=g_scl[c][:], in_=g_grp[c][:]
+                )
+            else:
+                nc.vector.quantize_mx(
+                    out=f_cod[c][:, a * 256 : (a + 1) * 256].bitcast(E4M3X4),
+                    scales=f_scl[c][:, a * 256 : (a + 1) * 256],
+                    in_=f_grp[c][:, a * 1024 : (a + 1) * 1024],
+                )
 
         count = [0, 0, 0, 0]
 
-        def multiply(c, m):
-            cols = slice(m * P, (m + 1) * P)
-            nc.tensor.matmul_mx(
-                out=acc[m][:],
-                lhsT=f_cod[c][:, cols].bitcast(E4M3X4),
-                lhsT_scale=f_scl[c][:, cols],
-                rhs=g_cod[c][:].bitcast(E5M2X4),
-                rhs_scale=g_scl[c][:],
-                start=(count[m] == 0),
-                stop=(count[m] == PASSES - 1),
-            )
-            count[m] += 1
+        def multiply(c, a):
+            for m in (2 * a, 2 * a + 1):
+                cols = slice(m * P, (m + 1) * P)
+                nc.tensor.matmul_mx(
+                    out=acc[m][:],
+                    lhsT=f_cod[c][:, cols].bitcast(E4M3X4),
+                    lhsT_scale=f_scl[c][:, cols],
+                    rhs=g_cod[c][:].bitcast(E5M2X4),
+                    rhs_scale=g_scl[c][:],
+                    start=(count[m] == 0),
+                    stop=(count[m] == PASSES - 1),
+                )
+                count[m] += 1
 
         ready = set()
         multiplied = set()
 
         def finish(item):
-            if item[0] == "g":
-                quantise_g(item[1])
-            else:
-                quantise_f(item[1], item[2] * 256, item[2] * 256 + 256)
+            quantise(item[0], item[1], item[2])
             ready.add(item)
             for c in range(PASSES):
                 for a in range(2):
                     if ("g", c, 0) in ready and ("f", c, a) in ready and (c, a) not in multiplied:
                         multiplied.add((c, a))
-                        multiply(c, 2 * a)
-                        multiply(c, 2 * a + 1)
+                        multiply(c, a)
 
         previous = None
-        for n, item in enumerate(LOADS[:-1]):
-            kind, c, a = item
-            if kind == "g":
-                regroup_g(nc.vector.tensor_copy, c, 0, 256)
-                regroup_g(nc.scalar.copy, c, 256, 512)
-            else:
-                regroup_f(nc.vector.tensor_copy, c, a, 0, 0, 8)
-                regroup_f(nc.scalar.copy, c, a, 1, 0, 8)
-            if n == 0:
-                finish(item)
-            else:
-                if previous is not None:
-                    finish(previous)
-                previous = item
-
-        kind, c, a = LOADS[-1]
-        regroup_f(nc.vector.tensor_copy, c, a, 0, 0, 4)
-        regroup_f(nc.vector.tensor_copy, c, a, 1, 0, 4)
-        regroup_f(nc.scalar.copy, c, a, 1, 4, 8)
+        for item in LOADS[:-1]:
+            regroup(item[0], item[1], item[2])
+            if previous is not None:
+                finish(previous)
+            previous = item
         finish(previous)
-        quantise_f(c, a * 256, a * 256 + 128)
-        multiply(c, 2 * a)
-        regroup_f(nc.vector.tensor_copy, c, a, 0, 4, 8)
-        quantise_f(c, a * 256 + 128, a * 256 + 256)
-        multiply(c, 2 * a + 1)
+        regroup(LOADS[-1][0], LOADS[-1][1], LOADS[-1][2])
+        finish(LOADS[-1])
 
-        for m in range(4):
-            if m < 3:
-                nc.scalar.copy(out=res[m][:], in_=acc[m][:])
-            else:
-                nc.vector.tensor_copy(out=res[m][:], in_=acc[m][:])
+        for m in range(2):
+            nc.scalar.copy(out=res[m][:], in_=acc[m][:])
             nc.sync.dma_start(out=out[m * P : (m + 1) * P, :], in_=res[m][:])
+        for half in range(2):
+            cols = slice(half * 256, (half + 1) * 256)
+            nc.scalar.copy(out=res[2][:, cols], in_=acc[2][:, cols])
+            nc.vector.tensor_copy(out=res[3][:, cols], in_=acc[3][:, cols])
+            for m in (2, 3):
+                nc.sync.dma_start(out=out[m * P : (m + 1) * P, cols], in_=res[m][:, cols])

@@ -18,7 +18,7 @@ F = 512
 FLOPS = 2 * 2048 * 512 * 512
 BYTES = 2 * 2048 * 512 * 2 + 512 * 512 * 4
 
-PINNED = True
+PINNED = False
 LOADS = (
     ("f", 0, 0), ("g", 0, 0), ("f", 1, 0), ("g", 1, 0), ("f", 2, 0), ("g", 2, 0), ("f", 3, 0), ("g", 3, 0),
     ("f", 0, 1), ("f", 1, 1), ("f", 2, 1), ("f", 3, 1),
@@ -118,21 +118,16 @@ def tile_resampling_kernel(tc, encoded, W, b, pos_emb, grad_out, out):
                         multiply(c, a)
 
         previous = None
-        for item in LOADS[:-1]:
+        for item in LOADS:
             regroup(item[0], item[1], item[2])
             if previous is not None:
                 finish(previous)
             previous = item
         finish(previous)
-        regroup(LOADS[-1][0], LOADS[-1][1], LOADS[-1][2])
-        finish(LOADS[-1])
 
-        for m in range(2):
-            nc.scalar.copy(out=res[m][:], in_=acc[m][:])
+        for m in range(4):
+            if m < 3:
+                nc.scalar.copy(out=res[m][:], in_=acc[m][:])
+            else:
+                nc.vector.tensor_copy(out=res[m][:], in_=acc[m][:])
             nc.sync.dma_start(out=out[m * P : (m + 1) * P, :], in_=res[m][:])
-        for half in range(2):
-            cols = slice(half * 256, (half + 1) * 256)
-            nc.scalar.copy(out=res[2][:, cols], in_=acc[2][:, cols])
-            nc.vector.tensor_copy(out=res[3][:, cols], in_=acc[3][:, cols])
-            for m in (2, 3):
-                nc.sync.dma_start(out=out[m * P : (m + 1) * P, cols], in_=res[m][:, cols])

@@ -20,7 +20,7 @@ BYTES = 2 * 2048 * 512 * 2 + 512 * 512 * 4
 
 PINNED = False
 LOADS = (
-    ("f", 0, 0), ("g", 0, 0), ("f", 1, 0), ("g", 1, 0), ("f", 2, 0), ("g", 2, 0), ("f", 3, 0), ("g", 3, 0),
+    ("f", 0, 0), ("f", 1, 0), ("f", 2, 0), ("f", 3, 0), ("g", 0, 0), ("g", 1, 0), ("g", 2, 0), ("g", 3, 0),
     ("f", 0, 1), ("f", 1, 1), ("f", 2, 1), ("f", 3, 1),
 )
 

@@ -18,10 +18,16 @@ F = 512
 FLOPS = 2 * 2048 * 512 * 512
 BYTES = 2 * 2048 * 512 * 2 + 512 * 512 * 4
 
-PINNED = False
 LOADS = (
     ("f", 0, 0), ("f", 1, 0), ("f", 2, 0), ("f", 3, 0), ("g", 0, 0), ("g", 1, 0), ("g", 2, 0), ("g", 3, 0),
     ("f", 0, 1), ("f", 1, 1), ("f", 2, 1), ("f", 3, 1),
+)
+STEPS = (
+    ("I", "f", 0, 1, 0), ("I", "f", 1, 1, 0), ("I", "f", 2, 1, 0), ("Q", "f", 0, 2, 0), ("I", "f", 3, 1, 0),
+    ("I", "g", 0, 1, 0), ("Q", "f", 2, 2, 0), ("I", "g", 1, 1, 0), ("Q", "g", 0, 1, 0), ("I", "g", 2, 1, 0),
+    ("Q", "g", 1, 1, 0), ("I", "g", 3, 1, 0), ("Q", "g", 2, 1, 0), ("I", "f", 0, 1, 1), ("Q", "g", 3, 1, 0),
+    ("I", "f", 1, 1, 1), ("Q", "f", 0, 1, 1), ("I", "f", 2, 1, 1), ("Q", "f", 1, 1, 1), ("I", "f", 3, 1, 1),
+    ("Q", "f", 2, 1, 1), ("Q", "f", 3, 1, 1),
 )
 
 
@@ -30,8 +36,6 @@ def tile_resampling_kernel(tc, encoded, W, b, pos_emb, grad_out, out):
     with ExitStack() as ctx:
         keep = ctx.enter_context(tc.tile_pool(name="keep", bufs=1))
         psum = ctx.enter_context(tc.psum_pool(name="acc", bufs=1))
-        if PINNED:
-            ctx.enter_context(tc.manual_schedule())
 
         enc_v = encoded.rearrange(
             "i (h y a x r) c -> i h a y x (r c)", h=2, y=16, a=2, x=8, r=8
@@ -39,91 +43,94 @@ def tile_resampling_kernel(tc, encoded, W, b, pos_emb, grad_out, out):
         g_v = grad_out.flatten_outer_dims().rearrange("(c p j) e -> c p (j e)", p=P, j=PACK)
 
         f_raw = [keep.tile([P, 2, 1024], BF16, name="f_raw%d" % c) for c in range(PASSES)]
-        g_raw = [keep.tile([P, 2048], BF16, name="g_raw%d" % c) for c in range(PASSES)]
-        f_grp = [keep.tile([P, 2048], BF16, name="f_grp%d" % c, align_bytes=64) for c in range(PASSES)]
-        g_grp = [keep.tile([P, 2048], BF16, name="g_grp%d" % c, align_bytes=64) for c in range(PASSES)]
-        f_cod = [keep.tile([P, D1], U32, name="f_cod%d" % c, align_bytes=64) for c in range(PASSES)]
-        g_cod = [keep.tile([P, F], U32, name="g_cod%d" % c, align_bytes=64) for c in range(PASSES)]
-        f_scl = [keep.tile([P, D1], U8, name="f_scl%d" % c, align_bytes=64) for c in range(PASSES)]
-        g_scl = [keep.tile([P, F], U8, name="g_scl%d" % c, align_bytes=64) for c in range(PASSES)]
+        g_raw = keep.tile([P, PASSES, 2048], BF16, name="g_raw")
+        f_grp = [keep.tile([P, PASSES * 1024], BF16, name="f_grp%d" % a, align_bytes=64) for a in range(2)]
+        g_grp = keep.tile([P, PASSES * 2048], BF16, name="g_grp", align_bytes=64)
+        f_cod = [keep.tile([P, PASSES * 256], U32, name="f_cod%d" % a, align_bytes=64) for a in range(2)]
+        g_cod = keep.tile([P, PASSES * F], U32, name="g_cod", align_bytes=64)
+        f_scl = [keep.tile([P, PASSES * 256], U8, name="f_scl%d" % a, align_bytes=64) for a in range(2)]
+        g_scl = keep.tile([P, PASSES * F], U8, name="g_scl", align_bytes=64)
         acc = [psum.tile([P, F], F32, name="acc%d" % m) for m in range(4)]
         res = [keep.tile([P, F], F32, name="res%d" % m) for m in range(4)]
 
         for kind, c, a in LOADS:
             if kind == "g":
-                nc.sync.dma_start(out=g_raw[c][:], in_=g_v[c])
+                nc.sync.dma_start(out=g_raw[:, c, :], in_=g_v[c])
             else:
                 nc.sync.dma_start(out=f_raw[c][:, a, :], in_=enc_v[c // 2, c % 2, a])
 
-        def regroup(kind, c, a):
-            if kind == "g":
-                src = g_raw[c][:].rearrange("p (j e) -> p j e", j=PACK)
-                for half, copy in ((0, nc.vector.tensor_copy), (1, nc.scalar.copy)):
+        def regroup_g(c, n):
+            src = g_raw[:, c : c + n, :].rearrange("p c (j e) -> p c j e", j=PACK)
+            dst = g_grp[:, c * 2048 : (c + n) * 2048].rearrange("p (c e j) -> p c e j", c=n, j=PACK)
+            for lo, hi, copy in ((0, 256, nc.vector.tensor_copy), (256, F, nc.scalar.copy)):
+                if n == 1:
                     copy(
-                        out=g_grp[c][:, half * 1024 : (half + 1) * 1024].rearrange(
-                            "p (q i j) -> p q j i", i=4, j=PACK
-                        ),
-                        in_=src[:, :, half * 256 : (half + 1) * 256].rearrange(
-                            "p j (q i) -> p q j i", i=4
-                        ),
+                        out=dst[:, 0, lo:hi, :].rearrange("p (q i) j -> p q j i", i=4),
+                        in_=src[:, 0, :, lo:hi].rearrange("p j (q i) -> p q j i", i=4),
                     )
-            else:
-                dst = f_grp[c][:, a * 1024 : (a + 1) * 1024].rearrange(
-                    "p (r b q i j) -> p b r q j i", r=8, b=2, q=4, i=4, j=PACK
-                )
-                src = f_raw[c][:, a, :].rearrange(
-                    "p (j b r q i) -> p b r q j i", r=8, b=2, q=4, i=4, j=PACK
-                )
-                nc.vector.tensor_copy(out=dst[:, 0], in_=src[:, 0])
-                nc.scalar.copy(out=dst[:, 1], in_=src[:, 1])
+                else:
+                    copy(
+                        out=dst[:, :, lo:hi, :].rearrange("p c (q i) j -> p c q j i", i=4),
+                        in_=src[:, :, :, lo:hi].rearrange("p c j (q i) -> p c q j i", i=4),
+                    )
 
-        def quantise(kind, c, a):
-            if kind == "g":
-                nc.vector.quantize_mx(
-                    out=g_cod[c][:].bitcast(E5M2X4), scales=g_scl[c][:], in_=g_grp[c][:]
-                )
-            else:
-                nc.vector.quantize_mx(
-                    out=f_cod[c][:, a * 256 : (a + 1) * 256].bitcast(E4M3X4),
-                    scales=f_scl[c][:, a * 256 : (a + 1) * 256],
-                    in_=f_grp[c][:, a * 1024 : (a + 1) * 1024],
-                )
+        def regroup_f(c, a):
+            dst = f_grp[a][:, c * 1024 : (c + 1) * 1024].rearrange(
+                "p (r b q i j) -> p b r q j i", r=8, b=2, q=4, i=4, j=PACK
+            )
+            src = f_raw[c][:, a, :].rearrange(
+                "p (j b r q i) -> p b r q j i", r=8, b=2, q=4, i=4, j=PACK
+            )
+            nc.vector.tensor_copy(out=dst[:, 0], in_=src[:, 0])
+            nc.scalar.copy(out=dst[:, 1], in_=src[:, 1])
 
         count = [0, 0, 0, 0]
 
-        def multiply(c, a):
-            for m in (2 * a, 2 * a + 1):
-                cols = slice(m * P, (m + 1) * P)
-                nc.tensor.matmul_mx(
-                    out=acc[m][:],
-                    lhsT=f_cod[c][:, cols].bitcast(E4M3X4),
-                    lhsT_scale=f_scl[c][:, cols],
-                    rhs=g_cod[c][:].bitcast(E5M2X4),
-                    rhs_scale=g_scl[c][:],
-                    start=(count[m] == 0),
-                    stop=(count[m] == PASSES - 1),
-                )
-                count[m] += 1
+        def multiply(c, m):
+            cols = slice(c * 256 + (m % 2) * P, c * 256 + (m % 2 + 1) * P)
+            nc.tensor.matmul_mx(
+                out=acc[m][:],
+                lhsT=f_cod[m // 2][:, cols].bitcast(E4M3X4),
+                lhsT_scale=f_scl[m // 2][:, cols],
+                rhs=g_cod[:, c * F : (c + 1) * F].bitcast(E5M2X4),
+                rhs_scale=g_scl[:, c * F : (c + 1) * F],
+                start=(count[m] == 0),
+                stop=(count[m] == PASSES - 1),
+            )
+            count[m] += 1
 
         ready = set()
         multiplied = set()
 
-        def finish(item):
-            quantise(item[0], item[1], item[2])
-            ready.add(item)
-            for c in range(PASSES):
-                for a in range(2):
-                    if ("g", c, 0) in ready and ("f", c, a) in ready and (c, a) not in multiplied:
-                        multiplied.add((c, a))
-                        multiply(c, a)
+        def quantise(kind, c, n, a):
+            if kind == "g":
+                nc.vector.quantize_mx(
+                    out=g_cod[:, c * F : (c + n) * F].bitcast(E5M2X4),
+                    scales=g_scl[:, c * F : (c + n) * F],
+                    in_=g_grp[:, c * 2048 : (c + n) * 2048],
+                )
+            else:
+                nc.vector.quantize_mx(
+                    out=f_cod[a][:, c * 256 : (c + n) * 256].bitcast(E4M3X4),
+                    scales=f_scl[a][:, c * 256 : (c + n) * 256],
+                    in_=f_grp[a][:, c * 1024 : (c + n) * 1024],
+                )
+            for k in range(c, c + n):
+                ready.add((kind, k, a))
+            for k in range(PASSES):
+                for half in range(2):
+                    if ("g", k, 0) in ready and ("f", k, half) in ready and (k, half) not in multiplied:
+                        multiplied.add((k, half))
+                        multiply(k, 2 * half)
+                        multiply(k, 2 * half + 1)
 
-        previous = None
-        for item in LOADS:
-            regroup(item[0], item[1], item[2])
-            if previous is not None:
-                finish(previous)
-            previous = item
-        finish(previous)
+        for what, kind, c, n, a in STEPS:
+            if what == "Q":
+                quantise(kind, c, n, a)
+            elif kind == "g":
+                regroup_g(c, n)
+            else:
+                regroup_f(c, a)
 
         for m in range(4):
             if m < 3:

@@ -26,8 +26,8 @@ STEPS = (
     ("I", "f", 0, 1, 0), ("I", "f", 1, 1, 0), ("I", "f", 2, 1, 0), ("Q", "f", 0, 2, 0), ("I", "f", 3, 1, 0),
     ("I", "g", 0, 1, 0), ("Q", "f", 2, 2, 0), ("I", "g", 1, 1, 0), ("Q", "g", 0, 1, 0), ("I", "g", 2, 1, 0),
     ("Q", "g", 1, 1, 0), ("I", "g", 3, 1, 0), ("Q", "g", 2, 1, 0), ("I", "f", 0, 1, 1), ("Q", "g", 3, 1, 0),
-    ("I", "f", 1, 1, 1), ("Q", "f", 0, 1, 1), ("I", "f", 2, 1, 1), ("Q", "f", 1, 1, 1), ("I", "f", 3, 1, 1),
-    ("Q", "f", 2, 1, 1), ("Q", "f", 3, 1, 1),
+    ("I", "f", 1, 1, 1), ("Q", "f", 0, 1, 1), ("I", "f", 2, 1, 1), ("Q", "f", 1, 1, 1), ("H", "f", 3, 0, 1),
+    ("Q", "f", 2, 1, 1), ("H", "f", 3, 1, 1), ("QH", "f", 3, 0, 1), ("QH", "f", 3, 1, 1),
 )
 
 
@@ -74,15 +74,24 @@ def tile_resampling_kernel(tc, encoded, W, b, pos_emb, grad_out, out):
                         in_=src[:, :, :, lo:hi].rearrange("p c j (q i) -> p c q j i", i=4),
                     )
 
-        def regroup_f(c, a):
+        def regroup_f(c, a, rows):
             dst = f_grp[a][:, c * 1024 : (c + 1) * 1024].rearrange(
                 "p (r b q i j) -> p b r q j i", r=8, b=2, q=4, i=4, j=PACK
             )
             src = f_raw[c][:, a, :].rearrange(
                 "p (j b r q i) -> p b r q j i", r=8, b=2, q=4, i=4, j=PACK
             )
-            nc.vector.tensor_copy(out=dst[:, 0], in_=src[:, 0])
-            nc.scalar.copy(out=dst[:, 1], in_=src[:, 1])
+            nc.vector.tensor_copy(out=dst[:, 0, rows], in_=src[:, 0, rows])
+            nc.scalar.copy(out=dst[:, 1, rows], in_=src[:, 1, rows])
+
+        def quantise_half(c, h, a):
+            cols = slice(c * 256 + h * P, c * 256 + (h + 1) * P)
+            nc.vector.quantize_mx(
+                out=f_cod[a][:, cols].bitcast(E4M3X4),
+                scales=f_scl[a][:, cols],
+                in_=f_grp[a][:, c * 1024 + h * 512 : c * 1024 + (h + 1) * 512],
+            )
+            multiply(c, 2 * a + h)
 
         count = [0, 0, 0, 0]
 
@@ -127,10 +136,14 @@ def tile_resampling_kernel(tc, encoded, W, b, pos_emb, grad_out, out):
         for what, kind, c, n, a in STEPS:
             if what == "Q":
                 quantise(kind, c, n, a)
+            elif what == "H":
+                regroup_f(c, a, slice(n * 4, n * 4 + 4))
+            elif what == "QH":
+                quantise_half(c, n, a)
             elif kind == "g":
                 regroup_g(c, n)
             else:
-                regroup_f(c, a)
+                regroup_f(c, a, slice(0, 8))
 
         for m in range(4):
             if m < 3:

@@ -65,8 +65,8 @@ def tile_resampling_kernel(tc, encoded, W, b, pos_emb, grad_out, out):
             for lo, hi, copy in ((0, 256, nc.vector.tensor_copy), (256, F, nc.scalar.copy)):
                 if n == 1:
                     copy(
-                        out=dst[:, 0, lo:hi, :].rearrange("p (q i) j -> p q j i", i=4),
-                        in_=src[:, 0, :, lo:hi].rearrange("p j (q i) -> p q j i", i=4),
+                        out=dst[:, 0, lo:hi, :].rearrange("p (q i) j -> p q j i", i=2),
+                        in_=src[:, 0, :, lo:hi].rearrange("p j (q i) -> p q j i", i=2),
                     )
                 else:
                     copy(
@@ -76,10 +76,10 @@ def tile_resampling_kernel(tc, encoded, W, b, pos_emb, grad_out, out):
 
         def regroup_f(c, a, rows):
             dst = f_grp[a][:, c * 1024 : (c + 1) * 1024].rearrange(
-                "p (r b q i j) -> p b r q j i", r=8, b=2, q=4, i=4, j=PACK
+                "p (r b q i j) -> p b r q j i", r=8, b=2, q=8, i=2, j=PACK
             )
             src = f_raw[c][:, a, :].rearrange(
-                "p (j b r q i) -> p b r q j i", r=8, b=2, q=4, i=4, j=PACK
+                "p (j b r q i) -> p b r q j i", r=8, b=2, q=8, i=2, j=PACK
             )
             nc.vector.tensor_copy(out=dst[:, 0, rows], in_=src[:, 0, rows])
             nc.scalar.copy(out=dst[:, 1, rows], in_=src[:, 1, rows])

from contextlib import ExitStack

import concourse.mybir as mybir

BF16 = mybir.dt.bfloat16
F32 = mybir.dt.float32
U32 = mybir.dt.uint32
U8 = mybir.dt.uint8
E4M3X4 = mybir.dt.float8_e4m3fn_x4
E5M2X4 = mybir.dt.float8_e5m2_x4

P = 128
PACK = 4
PASSES = 4
D1 = 512
F = 512

FLOPS = 2 * 2048 * 512 * 512
BYTES = 2 * 2048 * 512 * 2 + 512 * 512 * 4

LOADS = (
    ("f", 0, 0), ("f", 1, 0), ("f", 2, 0), ("f", 3, 0), ("g", 0, 0), ("g", 1, 0), ("g", 2, 0), ("g", 3, 0),
    ("f", 0, 1), ("f", 1, 1), ("f", 2, 1), ("f", 3, 1),
)
STEPS = (
    ("I", "f", 0, 1, 0), ("I", "f", 1, 1, 0), ("I", "f", 2, 1, 0), ("Q", "f", 0, 2, 0), ("I", "f", 3, 1, 0),
    ("I", "g", 0, 1, 0), ("Q", "f", 2, 2, 0), ("I", "g", 1, 1, 0), ("Q", "g", 0, 1, 0), ("I", "g", 2, 1, 0),
    ("Q", "g", 1, 1, 0), ("I", "g", 3, 1, 0), ("Q", "g", 2, 1, 0), ("I", "f", 0, 1, 1), ("Q", "g", 3, 1, 0),
    ("I", "f", 1, 1, 1), ("Q", "f", 0, 1, 1), ("I", "f", 2, 1, 1), ("Q", "f", 1, 1, 1), ("H", "f", 3, 0, 1),
    ("Q", "f", 2, 1, 1), ("H", "f", 3, 1, 1), ("QH", "f", 3, 0, 1), ("QH", "f", 3, 1, 1),
)


def tile_resampling_kernel(tc, encoded, W, b, pos_emb, grad_out, out):
    nc = tc.nc
    with ExitStack() as ctx:
        keep = ctx.enter_context(tc.tile_pool(name="keep", bufs=1))
        psum = ctx.enter_context(tc.psum_pool(name="acc", bufs=1))

        enc_v = encoded.rearrange(
            "i (h y a x r) c -> i h a y x (r c)", h=2, y=16, a=2, x=8, r=8
        )
        g_v = grad_out.flatten_outer_dims().rearrange("(c p j) e -> c p (j e)", p=P, j=PACK)

        f_raw = [keep.tile([P, 2, 1024], BF16, name="f_raw%d" % c) for c in range(PASSES)]
        g_raw = keep.tile([P, PASSES, 2048], BF16, name="g_raw")
        f_grp = [keep.tile([P, PASSES * 1024], BF16, name="f_grp%d" % a, align_bytes=64) for a in range(2)]
        g_grp = keep.tile([P, PASSES * 2048], BF16, name="g_grp", align_bytes=64)
        f_cod = [keep.tile([P, PASSES * 256], U32, name="f_cod%d" % a, align_bytes=64) for a in range(2)]
        g_cod = keep.tile([P, PASSES * F], U32, name="g_cod", align_bytes=64)
        f_scl = [keep.tile([P, PASSES * 256], U8, name="f_scl%d" % a, align_bytes=64) for a in range(2)]
        g_scl = keep.tile([P, PASSES * F], U8, name="g_scl", align_bytes=64)
        acc = [psum.tile([P, F], F32, name="acc%d" % m) for m in range(4)]
        res = [keep.tile([P, F], F32, name="res%d" % m) for m in range(4)]

        for kind, c, a in LOADS:
            if kind == "g":
                nc.sync.dma_start(out=g_raw[:, c, :], in_=g_v[c])
            else:
                nc.sync.dma_start(out=f_raw[c][:, a, :], in_=enc_v[c // 2, c % 2, a])

        def regroup_g(c, n):
            src = g_raw[:, c : c + n, :].rearrange("p c (j e) -> p c j e", j=PACK)
            dst = g_grp[:, c * 2048 : (c + n) * 2048].rearrange("p (c e j) -> p c e j", c=n, j=PACK)
            for lo, hi, copy in ((0, 256, nc.vector.tensor_copy), (256, F, nc.scalar.copy)):
                if n == 1:
                    copy(
                        out=dst[:, 0, lo:hi, :].rearrange("p (q i) j -> p q j i", i=2),
                        in_=src[:, 0, :, lo:hi].rearrange("p j (q i) -> p q j i", i=2),
                    )
                else:
                    copy(
                        out=dst[:, :, lo:hi, :].rearrange("p c (q i) j -> p c q j i", i=4),
                        in_=src[:, :, :, lo:hi].rearrange("p c j (q i) -> p c q j i", i=4),
                    )

        def regroup_f(c, a, rows):
            dst = f_grp[a][:, c * 1024 : (c + 1) * 1024].rearrange(
                "p (r b q i j) -> p b r q j i", r=8, b=2, q=8, i=2, j=PACK
            )
            src = f_raw[c][:, a, :].rearrange(
                "p (j b r q i) -> p b r q j i", r=8, b=2, q=8, i=2, j=PACK
            )
            nc.vector.tensor_copy(out=dst[:, 0, rows], in_=src[:, 0, rows])
            nc.scalar.copy(out=dst[:, 1, rows], in_=src[:, 1, rows])

        def quantise_half(c, h, a):
            cols = slice(c * 256 + h * P, c * 256 + (h + 1) * P)
            nc.vector.quantize_mx(
                out=f_cod[a][:, cols].bitcast(E4M3X4),
                scales=f_scl[a][:, cols],
                in_=f_grp[a][:, c * 1024 + h * 512 : c * 1024 + (h + 1) * 512],
            )
            multiply(c, 2 * a + h)

        count = [0, 0, 0, 0]

        def multiply(c, m):
            cols = slice(c * 256 + (m % 2) * P, c * 256 + (m % 2 + 1) * P)
            nc.tensor.matmul_mx(
                out=acc[m][:],
                lhsT=f_cod[m // 2][:, cols].bitcast(E4M3X4),
                lhsT_scale=f_scl[m // 2][:, cols],
                rhs=g_cod[:, c * F : (c + 1) * F].bitcast(E5M2X4),
                rhs_scale=g_scl[:, c * F : (c + 1) * F],
                start=(count[m] == 0),
                stop=(count[m] == PASSES - 1),
            )
            count[m] += 1

        ready = set()
        multiplied = set()

        def quantise(kind, c, n, a):
            if kind == "g":
                nc.vector.quantize_mx(
                    out=g_cod[:, c * F : (c + n) * F].bitcast(E5M2X4),
                    scales=g_scl[:, c * F : (c + n) * F],
                    in_=g_grp[:, c * 2048 : (c + n) * 2048],
                )
            else:
                nc.vector.quantize_mx(
                    out=f_cod[a][:, c * 256 : (c + n) * 256].bitcast(E4M3X4),
                    scales=f_scl[a][:, c * 256 : (c + n) * 256],
                    in_=f_grp[a][:, c * 1024 : (c + n) * 1024],
                )
            for k in range(c, c + n):
                ready.add((kind, k, a))
            for k in range(PASSES):
                for half in range(2):
                    if ("g", k, 0) in ready and ("f", k, half) in ready and (k, half) not in multiplied:
                        multiplied.add((k, half))
                        multiply(k, 2 * half)
                        multiply(k, 2 * half + 1)

        for what, kind, c, n, a in STEPS:
            if what == "Q":
                quantise(kind, c, n, a)
            elif what == "H":
                regroup_f(c, a, slice(n * 4, n * 4 + 4))
            elif what == "QH":
                quantise_half(c, n, a)
            elif kind == "g":
                regroup_g(c, n)
            else:
                regroup_f(c, a, slice(0, 8))

        for m in range(4):
            if m < 3:
                nc.scalar.copy(out=res[m][:], in_=acc[m][:])
            else:
                nc.vector.tensor_copy(out=res[m][:], in_=acc[m][:])
            nc.sync.dma_start(out=out[m * P : (m + 1) * P, :], in_=res[m][:])
